import numpy as np
import ml_dtypes


def mxq(x, axis, fmt="e4m3"):
    dtype, down = {"e4m3": (ml_dtypes.float8_e4m3fn, 7), "e5m2": (ml_dtypes.float8_e5m2, 14)}[fmt]
    v = np.moveaxis(np.asarray(x, np.float32).astype(ml_dtypes.bfloat16).astype(np.float64), axis, -1)
    blocks = v.reshape(v.shape[:-1] + (-1, 32))
    amax = np.abs(blocks).max(-1, keepdims=True)
    byte = np.maximum(np.where(amax > 0, np.frexp(amax)[1] - 1 + 127, 0) - down, 1)
    scale = np.exp2(byte - 127.0)
    codes = (blocks / scale).astype(np.float32).astype(dtype).astype(np.float64)
    return np.moveaxis((codes * scale).reshape(v.shape), -1, axis)


WIDE = False


def mx_kscale(k):
    if not WIDE:
        return np.ones(k)
    levels = np.array([10, -10, 5, -5, 0])
    a = np.random.permutation(np.resize(levels, k // 512 * 4)).reshape(k // 512, 4)
    idx = np.arange(k)
    return np.exp2(a[idx // 512, idx % 128 // 32])


BF16 = ml_dtypes.bfloat16


def bf(x):
    return np.asarray(x, np.float32).astype(BF16)


def f64(x):
    return np.asarray(x).astype(np.float64)


B, L, D, F, K = 128, 8, 8192, 64, 16
EPS = 1e-12


def silu(v):
    return v / (1.0 + np.exp(-v))


def l2norm(t, axis):
    n = np.sqrt((t * t).sum(axis=axis, keepdims=True))
    return t / np.maximum(n, EPS)


def mix_draw(rows, cols):
    return np.random.standard_normal((L, rows, cols)) * np.sqrt(np.e / K) * np.exp(0.5 * np.random.standard_normal((L, 1, cols)))


def gain_draw():
    return (1.0 + 0.1 * np.random.standard_normal((1, F))) * np.where(np.random.standard_normal((1, F)) < 0.0, -1.0, 1.0)


def setup_inputs():
    s = mx_kscale(D)
    g = np.sqrt(np.mean(1.0 / s**2))
    return {"x": bf(np.random.standard_normal((B, L, D)) * 3.0 / np.sqrt(D) * s * g),
            "w_gate_mix": bf(mix_draw(D, F) / s[:, None]),
            "w_up_mix": bf(mix_draw(D, F) / s[:, None]),
            "u_scale_param": bf(gain_draw()),
            "v_scale_param": bf(gain_draw())}


def reference(x, w_gate_mix, w_up_mix, u_scale_param, v_scale_param):
    wg = l2norm(f64(w_gate_mix), 1)
    wu = l2norm(f64(w_up_mix), 1)
    xq = mxq(f64(x).transpose(1, 0, 2), 2, "e4m3")
    u = xq @ mxq(wg, 1, "e4m3")
    v = xq @ mxq(wu, 1, "e4m3")
    u_scale = np.abs(f64(u_scale_param))
    v_scale = np.abs(f64(v_scale_param)) * np.sqrt(D)
    h = silu(v_scale * v) * (u_scale * u)
    return h.transpose(1, 0, 2)

@@ -1,0 +1,247 @@
+from contextlib import ExitStack
+import math
+
+import concourse.mybir as mybir
+from concourse.masks import make_identity
+
+F32 = mybir.dt.float32
+BF16 = mybir.dt.bfloat16
+U32 = mybir.dt.uint32
+U8 = mybir.dt.uint8
+FP8X4 = mybir.dt.float8_e4m3fn_x4
+ALU = mybir.AluOpType
+ACT = mybir.ActivationFunctionType
+
+P = 128
+BATCH, TOKENS, FEATURES, HIDDEN = 128, 8, 8192, 64
+MATS = 2
+PACK = 4
+PASSES = FEATURES // (P * PACK)
+HALF = PASSES // 2
+PAIRS = HIDDEN // 2
+PER_BANK = 4
+EPS = 1e-12
+
+FLOPS = 2 * BATCH * TOKENS * FEATURES * MATS * HIDDEN
+
+
+def tile_npertokenswishglu_basis_pa_k_kernel(
+    tc, x, w_gate_mix, w_up_mix, u_scale_param, v_scale_param, out
+):
+    nc = tc.nc
+    with ExitStack() as ctx:
+        consts = ctx.enter_context(tc.tile_pool(name="consts", bufs=1))
+        w_pool = ctx.enter_context(tc.tile_pool(name="w_pool", bufs=3))
+        x_pool = ctx.enter_context(tc.tile_pool(name="x_pool", bufs=2))
+        grouped_pool = ctx.enter_context(tc.tile_pool(name="grouped_pool", bufs=3))
+        mx_pool = ctx.enter_context(tc.tile_pool(name="mx_pool", bufs=2))
+        small = ctx.enter_context(tc.tile_pool(name="small", bufs=3))
+        psum_w = ctx.enter_context(tc.psum_pool(name="psum_w", bufs=3))
+        psum_x = ctx.enter_context(tc.psum_pool(name="psum_x", bufs=2))
+        psum_norm = ctx.enter_context(tc.psum_pool(name="psum_norm", bufs=2))
+        psum_acc = ctx.enter_context(tc.psum_pool(name="psum_acc", bufs=1))
+
+        warm = consts.tile([P, 1], F32)
+        nc.vector.memset(warm[:], 0.0)
+        nc.scalar.activation(out=warm[:], in_=warm[:], func=ACT.Silu)
+
+        ident = consts.tile([P, P], F32)
+        make_identity(nc, ident[:])
+        ones = consts.tile([P, P], F32)
+        nc.vector.memset(ones[:], 1.0)
+        minus_half = consts.tile([P, 2], F32)
+        nc.vector.memset(minus_half[:], -0.5)
+        fold_q = consts.tile([P, PAIRS], F32)
+        nc.vector.tensor_reduce(
+            out=fold_q[:],
+            in_=ident[:].rearrange("k (t q) -> k q t", q=PAIRS),
+            axis=mybir.AxisListType.X,
+            op=ALU.add,
+        )
+        fold = consts.tile([P, PACK, PAIRS], F32)
+        nc.vector.tensor_copy(
+            out=fold[:], in_=fold_q[:].unsqueeze(1).to_broadcast([P, PACK, PAIRS])
+        )
+
+        params = consts.tile([P, MATS, HIDDEN], BF16)
+        for g, param in enumerate((u_scale_param, v_scale_param)):
+            nc.scalar.dma_start(
+                out=params[:, g, :],
+                in_=param.rearrange("o f -> (o f)").partition_broadcast(P),
+            )
+        gains = consts.tile([P, MATS, HIDDEN], F32)
+        nc.vector.scalar_tensor_tensor(
+            out=gains[:], in0=params[:], scalar=-1.0, in1=params[:], op0=ALU.mult, op1=ALU.max
+        )
+        nc.vector.tensor_scalar_mul(
+            out=gains[:, 1, :], in0=gains[:, 1, :], scalar1=math.sqrt(FEATURES)
+        )
+
+        w_raw_of = {}
+        x_raw_of = {}
+        inv_norm_of = {}
+        x_mx_of = {}
+
+        def load(l):
+            w_raw = w_pool.tile([P, MATS, PASSES, PACK * HIDDEN], BF16)
+            for g, w in enumerate((w_gate_mix, w_up_mix)):
+                nc.sync.dma_start(
+                    out=w_raw[:, g, :, :],
+                    in_=w[l, :, :].rearrange("(c p t) f -> p c (t f)", p=P, t=PACK),
+                )
+            x_raw = x_pool.tile([P, FEATURES], BF16)
+            nc.sync.dma_start(out=x_raw[:], in_=x[:, l, :])
+            w_raw_of[l] = w_raw
+            x_raw_of[l] = x_raw
+
+        def column_norms(l, g):
+            words = w_raw_of[l][:].bitcast(F32)
+            partial = small.tile([P, 2, PASSES // PER_BANK], F32)
+            for b in range(PASSES // PER_BANK):
+                w_t = psum_w.tile([P, PER_BANK, P], F32)
+                for i in range(PER_BANK):
+                    nc.tensor.transpose(w_t[:, i, :], words[:, g, PER_BANK * b + i, :], ident[:])
+                by_parity = w_t[:].bitcast(BF16).rearrange("k i (p e) -> k e i p", e=2)
+                for e in range(2):
+                    squares = small.tile([P, PER_BANK, P], BF16)
+                    nc.scalar.activation(
+                        out=squares[:],
+                        in_=by_parity[:, e, :, :],
+                        func=ACT.Square,
+                        accum_out=partial[:, e, b : b + 1],
+                    )
+            norm_ps = psum_norm.tile([P, 2 * HIDDEN], F32)
+            n_partial = 2 * (PASSES // PER_BANK)
+            nc.tensor.matmul(
+                out=norm_ps[:, 0:n_partial],
+                lhsT=fold[:].rearrange("k t q -> k (t q)"),
+                rhs=partial[:].rearrange("k e b -> k (e b)"),
+                start=True,
+                stop=True,
+            )
+            sum_sq = small.tile([P, 2], F32)
+            nc.vector.tensor_reduce(
+                out=sum_sq[:],
+                in_=norm_ps[:, 0:n_partial].rearrange("k (e b) -> k e b", e=2),
+                axis=mybir.AxisListType.X,
+                op=ALU.add,
+            )
+            floored = small.tile([P, 2], F32)
+            nc.gpsimd.tensor_scalar_max(out=floored[:], in0=sum_sq[:], scalar1=EPS * EPS)
+            inv = small.tile([P, 2], F32)
+            nc.gpsimd.tensor_tensor(out=inv[:], in0=floored[:], in1=minus_half[:], op=ALU.pow)
+            diag = small.tile([P, PAIRS, 2], F32)
+            nc.gpsimd.tensor_tensor(
+                out=diag[:],
+                in0=ident[:, 0:PAIRS].unsqueeze(2).to_broadcast([P, PAIRS, 2]),
+                in1=inv[:].unsqueeze(1).to_broadcast([P, PAIRS, 2]),
+                op=ALU.mult,
+            )
+            nc.tensor.matmul(
+                out=norm_ps[:, HIDDEN : 2 * HIDDEN],
+                lhsT=ones[:],
+                rhs=diag[:].rearrange("k q e -> k (q e)"),
+                start=True,
+                stop=True,
+            )
+            inv_norm = small.tile([P, HIDDEN], F32, bufs=6)
+            nc.vector.tensor_copy(out=inv_norm[:], in_=norm_ps[:, HIDDEN : 2 * HIDDEN])
+            inv_norm_of[l, g] = inv_norm
+
+        def quantise_x(l):
+            words = x_raw_of[l][:].bitcast(F32)
+            x_codes = mx_pool.tile([P, PASSES, BATCH], U32, align_bytes=64)
+            x_scales = mx_pool.tile([P, PASSES, BATCH], U8, align_bytes=64)
+            for h in range(2):
+                x_grouped = grouped_pool.tile([P, HALF, BATCH, PACK], BF16, align_bytes=64)
+                grouped_words = x_grouped[:].bitcast(F32)
+                for j in range(HALF // 2):
+                    x_t = psum_x.tile([P, 2, 2, BATCH], F32)
+                    for i in range(2):
+                        first = 2 * P * (h * HALF + 2 * j + i)
+                        for u in range(2):
+                            nc.tensor.transpose(
+                                x_t[:, i, u, :], words[:, first + u : first + 2 * P : 2], ident[:]
+                            )
+                    nc.scalar.copy(
+                        out=grouped_words[:, 2 * j : 2 * j + 2, :, :],
+                        in_=x_t[:].rearrange("p i u b -> p i b u"),
+                    )
+                passes = slice(h * HALF, (h + 1) * HALF)
+                nc.vector.quantize_mx(
+                    out=x_codes[:, passes, :].rearrange("p c b -> p (c b)").bitcast(FP8X4),
+                    scales=x_scales[:, passes, :].rearrange("p c b -> p (c b)"),
+                    in_=x_grouped[:].rearrange("p c b t -> p (c b t)"),
+                )
+            x_mx_of[l] = (x_codes, x_scales)
+
+        def token_output(l):
+            w_raw = w_raw_of[l]
+            w_codes = mx_pool.tile([P, PASSES, MATS * HIDDEN], U32, align_bytes=64)
+            w_scales = mx_pool.tile([P, PASSES, MATS * HIDDEN], U8, align_bytes=64)
+            w_grouped_of = []
+            for h in range(2):
+                w_grouped = grouped_pool.tile(
+                    [P, HALF, MATS, HIDDEN, PACK], BF16, align_bytes=64, bufs=4
+                )
+                w_grouped_of.append(w_grouped)
+            for g in range(MATS):
+                for h in range(2):
+                    nc.vector.tensor_tensor(
+                        out=w_grouped_of[h][:, :, g, :, :],
+                        in0=w_raw[:, g, h * HALF : (h + 1) * HALF, :].rearrange(
+                            "p c (t f) -> p c f t", t=PACK
+                        ),
+                        in1=inv_norm_of[l, g][:]
+                        .unsqueeze(1)
+                        .unsqueeze(3)
+                        .to_broadcast([P, HALF, HIDDEN, PACK]),
+                        op=ALU.mult,
+                    )
+            for h in range(2):
+                passes = slice(h * HALF, (h + 1) * HALF)
+                nc.vector.quantize_mx(
+                    out=w_codes[:, passes, :].rearrange("p c n -> p (c n)").bitcast(FP8X4),
+                    scales=w_scales[:, passes, :].rearrange("p c n -> p (c n)"),
+                    in_=w_grouped_of[h][:].rearrange("p c g f t -> p (c g f t)"),
+                )
+            x_codes, x_scales = x_mx_of[l]
+            acc = psum_acc.tile([BATCH, MATS * HIDDEN], F32)
+            for c in range(PASSES):
+                nc.tensor.matmul_mx(
+                    out=acc[:],
+                    lhsT=x_codes[:, c, :].bitcast(FP8X4),
+                    lhsT_scale=x_scales[:, c, :],
+                    rhs=w_codes[:, c, :].bitcast(FP8X4),
+                    rhs_scale=w_scales[:, c, :],
+                    start=(c == 0),
+                    stop=(c == PASSES - 1),
+                )
+            scaled = small.tile([BATCH, MATS, HIDDEN], F32)
+            nc.vector.tensor_tensor(
+                out=scaled[:],
+                in0=acc[:].rearrange("b (g f) -> b g f", g=MATS),
+                in1=gains[:],
+                op=ALU.mult,
+            )
+            silu_v = small.tile([BATCH, HIDDEN], F32)
+            nc.scalar.activation(out=silu_v[:], in_=scaled[:, 1, :], func=ACT.Silu)
+            result = small.tile([BATCH, HIDDEN], F32)
+            nc.gpsimd.tensor_tensor(
+                out=result[:], in0=silu_v[:], in1=scaled[:, 0, :], op=ALU.mult
+            )
+            nc.sync.dma_start(out=out[:, l, :], in_=result[:])
+
+        load(0)
+        load(1)
+        for g in range(MATS):
+            column_norms(0, g)
+        quantise_x(0)
+        for l in range(TOKENS):
+            if l + 2 < TOKENS:
+                load(l + 2)
+            if l + 1 < TOKENS:
+                for g in range(MATS):
+                    column_norms(l + 1, g)
+                quantise_x(l + 1)
+            token_output(l)

@@ -15,11 +15,17 @@ ACT = mybir.ActivationFunctionType
 P = 128
 BATCH, TOKENS, FEATURES, HIDDEN = 128, 8, 8192, 64
 MATS = 2
+UNITS = TOKENS * MATS
 PACK = 4
 PASSES = FEATURES // (P * PACK)
 HALF = PASSES // 2
-PAIRS = HIDDEN // 2
+HIDDEN_PAIRS = HIDDEN // 2
 PER_BANK = 4
+BANKS = PASSES // PER_BANK
+ALL_BANKS = UNITS * BANKS
+AHEAD = 2
+LOADED_AHEAD = 6
+GPSIMD_PASSES = 4
 EPS = 1e-12
 
 FLOPS = 2 * BATCH * TOKENS * FEATURES * MATS * HIDDEN
@@ -31,13 +37,11 @@ def tile_npertokenswishglu_basis_pa_k_kernel(
     nc = tc.nc
     with ExitStack() as ctx:
         consts = ctx.enter_context(tc.tile_pool(name="consts", bufs=1))
-        w_pool = ctx.enter_context(tc.tile_pool(name="w_pool", bufs=3))
-        x_pool = ctx.enter_context(tc.tile_pool(name="x_pool", bufs=2))
-        grouped_pool = ctx.enter_context(tc.tile_pool(name="grouped_pool", bufs=3))
+        raw_pool = ctx.enter_context(tc.tile_pool(name="raw_pool", bufs=LOADED_AHEAD))
+        grouped_pool = ctx.enter_context(tc.tile_pool(name="grouped_pool", bufs=4))
         mx_pool = ctx.enter_context(tc.tile_pool(name="mx_pool", bufs=2))
         small = ctx.enter_context(tc.tile_pool(name="small", bufs=3))
-        psum_w = ctx.enter_context(tc.psum_pool(name="psum_w", bufs=3))
-        psum_x = ctx.enter_context(tc.psum_pool(name="psum_x", bufs=2))
+        psum_t = ctx.enter_context(tc.psum_pool(name="psum_t", bufs=2 * AHEAD + 1))
         psum_norm = ctx.enter_context(tc.psum_pool(name="psum_norm", bufs=2))
         psum_acc = ctx.enter_context(tc.psum_pool(name="psum_acc", bufs=1))
 
@@ -51,16 +55,16 @@ def tile_npertokenswishglu_basis_pa_k_kernel(
         nc.vector.memset(ones[:], 1.0)
         minus_half = consts.tile([P, 2], F32)
         nc.vector.memset(minus_half[:], -0.5)
-        fold_q = consts.tile([P, PAIRS], F32)
+        fold_q = consts.tile([P, HIDDEN_PAIRS], F32)
         nc.vector.tensor_reduce(
             out=fold_q[:],
-            in_=ident[:].rearrange("k (t q) -> k q t", q=PAIRS),
+            in_=ident[:].rearrange("k (t q) -> k q t", q=HIDDEN_PAIRS),
             axis=mybir.AxisListType.X,
             op=ALU.add,
         )
-        fold = consts.tile([P, PACK, PAIRS], F32)
+        fold = consts.tile([P, PACK, HIDDEN_PAIRS], F32)
         nc.vector.tensor_copy(
-            out=fold[:], in_=fold_q[:].unsqueeze(1).to_broadcast([P, PACK, PAIRS])
+            out=fold[:], in_=fold_q[:].unsqueeze(1).to_broadcast([P, PACK, HIDDEN_PAIRS])
         )
 
         params = consts.tile([P, MATS, HIDDEN], BF16)
@@ -77,52 +81,102 @@ def tile_npertokenswishglu_basis_pa_k_kernel(
             out=gains[:, 1, :], in0=gains[:, 1, :], scalar1=math.sqrt(FEATURES)
         )
 
-        w_raw_of = {}
-        x_raw_of = {}
-        inv_norm_of = {}
-        x_mx_of = {}
+        w_raw_of, x_raw_of = {}, {}
+        w_bank_of, x_bank_of = {}, {}
+        partial_of, norm_ps_of, diag_of, inv_norm_of = {}, {}, {}, {}
+        x_grouped_of, w_grouped_of = {}, {}
+        x_mx_of, w_mx_of = {}, {}
+        acc_of, scaled_of = {}, {}
 
-        def load(l):
-            w_raw = w_pool.tile([P, MATS, PASSES, PACK * HIDDEN], BF16)
-            for g, w in enumerate((w_gate_mix, w_up_mix)):
+        def load(unit):
+            token, g = divmod(unit, MATS)
+            w = (w_gate_mix, w_up_mix)[g]
+            w_rows = w[token, :, :].rearrange("(c p t) f -> p c (t f)", p=P, t=PACK)
+            w_raw = raw_pool.tile([P, PASSES, PACK * HIDDEN], BF16)
+            x_raw = raw_pool.tile([P, FEATURES // 2], BF16)
+            piece = FEATURES // 2 // BANKS
+            for b in range(BANKS):
+                passes = slice(PER_BANK * b, PER_BANK * (b + 1))
+                nc.sync.dma_start(out=w_raw[:, passes, :], in_=w_rows[:, passes, :])
+                first = g * (FEATURES // 2) + b * piece
                 nc.sync.dma_start(
-                    out=w_raw[:, g, :, :],
-                    in_=w[l, :, :].rearrange("(c p t) f -> p c (t f)", p=P, t=PACK),
+                    out=x_raw[:, b * piece : (b + 1) * piece],
+                    in_=x[:, token, first : first + piece],
                 )
-            x_raw = x_pool.tile([P, FEATURES], BF16)
-            nc.sync.dma_start(out=x_raw[:], in_=x[:, l, :])
-            w_raw_of[l] = w_raw
-            x_raw_of[l] = x_raw
+            w_raw_of[unit] = w_raw
+            x_raw_of[unit] = x_raw
 
-        def column_norms(l, g):
-            words = w_raw_of[l][:].bitcast(F32)
-            partial = small.tile([P, 2, PASSES // PER_BANK], F32)
-            for b in range(PASSES // PER_BANK):
-                w_t = psum_w.tile([P, PER_BANK, P], F32)
-                for i in range(PER_BANK):
-                    nc.tensor.transpose(w_t[:, i, :], words[:, g, PER_BANK * b + i, :], ident[:])
-                by_parity = w_t[:].bitcast(BF16).rearrange("k i (p e) -> k e i p", e=2)
-                for e in range(2):
-                    squares = small.tile([P, PER_BANK, P], BF16)
-                    nc.scalar.activation(
-                        out=squares[:],
-                        in_=by_parity[:, e, :, :],
-                        func=ACT.Square,
-                        accum_out=partial[:, e, b : b + 1],
+        def fill_w(bank):
+            unit, b = divmod(bank, BANKS)
+            words = w_raw_of[unit][:].bitcast(F32)
+            w_bank = psum_t.tile([P, PER_BANK, P], F32, tag="bank")
+            for i in range(PER_BANK):
+                nc.tensor.transpose(w_bank[:, i, :], words[:, PER_BANK * b + i, :], ident[:])
+            w_bank_of[bank] = w_bank
+
+        def square_w(bank):
+            unit, b = divmod(bank, BANKS)
+            if b == 0:
+                partial = small.tile([P, 2, BANKS], F32)
+                partial_of[unit] = partial
+            by_parity = w_bank_of[bank][:].bitcast(BF16).rearrange("k i (p e) -> k e i p", e=2)
+            for e in range(2):
+                squares = small.tile([P, PER_BANK, P], BF16)
+                nc.scalar.activation(
+                    out=squares[:],
+                    in_=by_parity[:, e, :, :],
+                    func=ACT.Square,
+                    accum_out=partial_of[unit][:, e, b : b + 1],
+                )
+
+        def fill_x(bank):
+            unit, b = divmod(bank, BANKS)
+            words = x_raw_of[unit][:].bitcast(F32)
+            x_bank = psum_t.tile([P, PER_BANK, BATCH], F32, tag="bank")
+            for i in range(PER_BANK // 2):
+                first = 2 * P * (b * (PER_BANK // 2) + i)
+                for j in range(2):
+                    nc.tensor.transpose(
+                        x_bank[:, 2 * i + j, :], words[:, first + j : first + 2 * P : 2], ident[:]
                     )
+            x_bank_of[bank] = x_bank
+
+        def copy_x(bank):
+            unit, b = divmod(bank, BANKS)
+            if b == 0:
+                x_grouped = grouped_pool.tile([P, HALF, BATCH, PACK], BF16, align_bytes=64)
+                x_grouped_of[unit] = x_grouped
+            passes = slice(b * (PER_BANK // 2), (b + 1) * (PER_BANK // 2))
+            nc.scalar.copy(
+                out=x_grouped_of[unit][:].bitcast(F32)[:, passes, :, :],
+                in_=x_bank_of[bank][:].rearrange("p (i j) b -> p i b j", j=2),
+            )
+
+        def banks(first, count):
+            for bank in range(first, first + count):
+                if bank + AHEAD < ALL_BANKS:
+                    fill_w(bank + AHEAD)
+                square_w(bank)
+                if bank + AHEAD < ALL_BANKS:
+                    fill_x(bank + AHEAD)
+                copy_x(bank)
+
+        def fold_partial_sums(unit):
             norm_ps = psum_norm.tile([P, 2 * HIDDEN], F32)
-            n_partial = 2 * (PASSES // PER_BANK)
             nc.tensor.matmul(
-                out=norm_ps[:, 0:n_partial],
+                out=norm_ps[:, 0 : 2 * BANKS],
                 lhsT=fold[:].rearrange("k t q -> k (t q)"),
-                rhs=partial[:].rearrange("k e b -> k (e b)"),
+                rhs=partial_of[unit][:].rearrange("k e b -> k (e b)"),
                 start=True,
                 stop=True,
             )
+            norm_ps_of[unit] = norm_ps
+
+        def inverse_norms(unit):
             sum_sq = small.tile([P, 2], F32)
             nc.vector.tensor_reduce(
                 out=sum_sq[:],
-                in_=norm_ps[:, 0:n_partial].rearrange("k (e b) -> k e b", e=2),
+                in_=norm_ps_of[unit][:, 0 : 2 * BANKS].rearrange("k (e b) -> k e b", e=2),
                 axis=mybir.AxisListType.X,
                 op=ALU.add,
             )
@@ -130,82 +184,69 @@ def tile_npertokenswishglu_basis_pa_k_kernel(
             nc.gpsimd.tensor_scalar_max(out=floored[:], in0=sum_sq[:], scalar1=EPS * EPS)
             inv = small.tile([P, 2], F32)
             nc.gpsimd.tensor_tensor(out=inv[:], in0=floored[:], in1=minus_half[:], op=ALU.pow)
-            diag = small.tile([P, PAIRS, 2], F32)
+            diag = small.tile([P, HIDDEN_PAIRS, 2], F32)
             nc.gpsimd.tensor_tensor(
                 out=diag[:],
-                in0=ident[:, 0:PAIRS].unsqueeze(2).to_broadcast([P, PAIRS, 2]),
-                in1=inv[:].unsqueeze(1).to_broadcast([P, PAIRS, 2]),
+                in0=ident[:, 0:HIDDEN_PAIRS].unsqueeze(2).to_broadcast([P, HIDDEN_PAIRS, 2]),
+                in1=inv[:].unsqueeze(1).to_broadcast([P, HIDDEN_PAIRS, 2]),
                 op=ALU.mult,
             )
+            diag_of[unit] = diag
+
+        def spread_inverse_norms(unit):
+            spread = norm_ps_of[unit][:, HIDDEN : 2 * HIDDEN]
             nc.tensor.matmul(
-                out=norm_ps[:, HIDDEN : 2 * HIDDEN],
+                out=spread,
                 lhsT=ones[:],
-                rhs=diag[:].rearrange("k q e -> k (q e)"),
+                rhs=diag_of[unit][:].rearrange("k q e -> k (q e)"),
                 start=True,
                 stop=True,
             )
-            inv_norm = small.tile([P, HIDDEN], F32, bufs=6)
-            nc.vector.tensor_copy(out=inv_norm[:], in_=norm_ps[:, HIDDEN : 2 * HIDDEN])
-            inv_norm_of[l, g] = inv_norm
+            inv_norm = small.tile([P, HIDDEN], F32)
+            nc.vector.tensor_copy(out=inv_norm[:], in_=spread)
+            inv_norm_of[unit] = inv_norm
 
-        def quantise_x(l):
-            words = x_raw_of[l][:].bitcast(F32)
-            x_codes = mx_pool.tile([P, PASSES, BATCH], U32, align_bytes=64)
-            x_scales = mx_pool.tile([P, PASSES, BATCH], U8, align_bytes=64)
-            for h in range(2):
-                x_grouped = grouped_pool.tile([P, HALF, BATCH, PACK], BF16, align_bytes=64)
-                grouped_words = x_grouped[:].bitcast(F32)
-                for j in range(HALF // 2):
-                    x_t = psum_x.tile([P, 2, 2, BATCH], F32)
-                    for i in range(2):
-                        first = 2 * P * (h * HALF + 2 * j + i)
-                        for u in range(2):
-                            nc.tensor.transpose(
-                                x_t[:, i, u, :], words[:, first + u : first + 2 * P : 2], ident[:]
-                            )
-                    nc.scalar.copy(
-                        out=grouped_words[:, 2 * j : 2 * j + 2, :, :],
-                        in_=x_t[:].rearrange("p i u b -> p i b u"),
-                    )
-                passes = slice(h * HALF, (h + 1) * HALF)
-                nc.vector.quantize_mx(
-                    out=x_codes[:, passes, :].rearrange("p c b -> p (c b)").bitcast(FP8X4),
-                    scales=x_scales[:, passes, :].rearrange("p c b -> p (c b)"),
-                    in_=x_grouped[:].rearrange("p c b t -> p (c b t)"),
-                )
-            x_mx_of[l] = (x_codes, x_scales)
+        def normalise(engine, inv_norm, unit, first, count):
+            token, g = divmod(unit, MATS)
+            h, c = divmod(first, HALF)
+            engine.tensor_tensor(
+                out=w_grouped_of[token, h][:, c : c + count, g, :, :],
+                in0=w_raw_of[unit][:, first : first + count, :].rearrange(
+                    "p c (t f) -> p c f t", t=PACK
+                ),
+                in1=inv_norm.unsqueeze(1).unsqueeze(3).to_broadcast([P, count, HIDDEN, PACK]),
+                op=ALU.mult,
+            )
 
-        def token_output(l):
-            w_raw = w_raw_of[l]
+        def quantise_x(unit):
+            token, h = divmod(unit, MATS)
+            if h == 0:
+                x_codes = mx_pool.tile([P, PASSES, BATCH], U32, align_bytes=64)
+                x_scales = mx_pool.tile([P, PASSES, BATCH], U8, align_bytes=64)
+                x_mx_of[token] = (x_codes, x_scales)
+            x_codes, x_scales = x_mx_of[token]
+            passes = slice(h * HALF, (h + 1) * HALF)
+            nc.vector.quantize_mx(
+                out=x_codes[:, passes, :].rearrange("p c b -> p (c b)").bitcast(FP8X4),
+                scales=x_scales[:, passes, :].rearrange("p c b -> p (c b)"),
+                in_=x_grouped_of[unit][:].rearrange("p c b t -> p (c b t)"),
+            )
+
+        def quantise_w(token):
             w_codes = mx_pool.tile([P, PASSES, MATS * HIDDEN], U32, align_bytes=64)
             w_scales = mx_pool.tile([P, PASSES, MATS * HIDDEN], U8, align_bytes=64)
-            w_grouped_of = []
-            for h in range(2):
-                w_grouped = grouped_pool.tile(
-                    [P, HALF, MATS, HIDDEN, PACK], BF16, align_bytes=64, bufs=4
-                )
-                w_grouped_of.append(w_grouped)
-            for g in range(MATS):
-                for h in range(2):
-                    nc.vector.tensor_tensor(
-                        out=w_grouped_of[h][:, :, g, :, :],
-                        in0=w_raw[:, g, h * HALF : (h + 1) * HALF, :].rearrange(
-                            "p c (t f) -> p c f t", t=PACK
-                        ),
-                        in1=inv_norm_of[l, g][:]
-                        .unsqueeze(1)
-                        .unsqueeze(3)
-                        .to_broadcast([P, HALF, HIDDEN, PACK]),
-                        op=ALU.mult,
-                    )
             for h in range(2):
                 passes = slice(h * HALF, (h + 1) * HALF)
                 nc.vector.quantize_mx(
                     out=w_codes[:, passes, :].rearrange("p c n -> p (c n)").bitcast(FP8X4),
                     scales=w_scales[:, passes, :].rearrange("p c n -> p (c n)"),
-                    in_=w_grouped_of[h][:].rearrange("p c g f t -> p (c g f t)"),
+                    in_=w_grouped_of[token, h][:].rearrange("p c g f t -> p (c g f t)"),
                 )
-            x_codes, x_scales = x_mx_of[l]
+            w_mx_of[token] = (w_codes, w_scales)
+
+        def multiply(token):
+            x_codes, x_scales = x_mx_of[token]
+            w_codes, w_scales = w_mx_of[token]
             acc = psum_acc.tile([BATCH, MATS * HIDDEN], F32)
             for c in range(PASSES):
                 nc.tensor.matmul_mx(
@@ -217,31 +258,75 @@ def tile_npertokenswishglu_basis_pa_k_kernel(
                     start=(c == 0),
                     stop=(c == PASSES - 1),
                 )
+            acc_of[token] = acc
+
+        def apply_gains(token):
             scaled = small.tile([BATCH, MATS, HIDDEN], F32)
             nc.vector.tensor_tensor(
                 out=scaled[:],
-                in0=acc[:].rearrange("b (g f) -> b g f", g=MATS),
+                in0=acc_of[token][:].rearrange("b (g f) -> b g f", g=MATS),
                 in1=gains[:],
                 op=ALU.mult,
             )
+            scaled_of[token] = scaled
+
+        def finish(token):
+            scaled = scaled_of[token]
             silu_v = small.tile([BATCH, HIDDEN], F32)
             nc.scalar.activation(out=silu_v[:], in_=scaled[:, 1, :], func=ACT.Silu)
             result = small.tile([BATCH, HIDDEN], F32)
             nc.gpsimd.tensor_tensor(
                 out=result[:], in0=silu_v[:], in1=scaled[:, 0, :], op=ALU.mult
             )
-            nc.sync.dma_start(out=out[:, l, :], in_=result[:])
+            nc.sync.dma_start(out=out[:, token, :], in_=result[:])
 
-        load(0)
-        load(1)
-        for g in range(MATS):
-            column_norms(0, g)
-        quantise_x(0)
-        for l in range(TOKENS):
-            if l + 2 < TOKENS:
-                load(l + 2)
-            if l + 1 < TOKENS:
-                for g in range(MATS):
-                    column_norms(l + 1, g)
-                quantise_x(l + 1)
-            token_output(l)
+        def pipeline():
+            for unit in range(LOADED_AHEAD):
+                load(unit)
+            for bank in range(AHEAD):
+                fill_w(bank)
+                fill_x(bank)
+            for step in range(UNITS + 3):
+                measuring = step < UNITS
+                normalising = 1 <= step <= UNITS
+                unit = step - 1
+                token, g = divmod(unit, MATS)
+
+                if measuring:
+                    banks(step * BANKS, BANKS // 2)
+                if normalising:
+                    spread_inverse_norms(unit)
+                if step >= 4 and g == 1:
+                    finish(token - 1)
+                if measuring:
+                    banks(step * BANKS + BANKS // 2, BANKS // 2)
+                    fold_partial_sums(step)
+                if step >= 3 and g == 0:
+                    multiply(token - 1)
+                if normalising:
+                    if g == 0:
+                        for h in range(2):
+                            w_grouped = grouped_pool.tile(
+                                [P, HALF, MATS, HIDDEN, PACK], BF16, align_bytes=64
+                            )
+                            w_grouped_of[token, h] = w_grouped
+                    in_psum = norm_ps_of[unit][:, HIDDEN : 2 * HIDDEN]
+                    normalise(nc.vector, in_psum, unit, 0, HALF - GPSIMD_PASSES)
+                    normalise(
+                        nc.gpsimd, inv_norm_of[unit][:], unit, HALF - GPSIMD_PASSES, GPSIMD_PASSES
+                    )
+                if measuring:
+                    inverse_norms(step)
+                if normalising:
+                    normalise(nc.vector, in_psum, unit, HALF, HALF)
+                if step >= 3 and g == 0:
+                    apply_gains(token - 1)
+                if normalising:
+                    quantise_x(unit)
+                    if g == 1:
+                        quantise_w(token)
+                    if unit + LOADED_AHEAD < UNITS:
+                        load(unit + LOADED_AHEAD)
+
+        with tc.manual_schedule():
+            pipeline()

@@ -22,8 +22,7 @@ HALF = PASSES // 2
 HIDDEN_PAIRS = HIDDEN // 2
 PER_BANK = 4
 BANKS = PASSES // PER_BANK
-ALL_BANKS = UNITS * BANKS
-AHEAD = 2
+VECTOR_COPIES = 2
 LOADED_AHEAD = 6
 GPSIMD_PASSES = 4
 EPS = 1e-12
@@ -41,7 +40,7 @@ def tile_npertokenswishglu_basis_pa_k_kernel(
         grouped_pool = ctx.enter_context(tc.tile_pool(name="grouped_pool", bufs=4))
         mx_pool = ctx.enter_context(tc.tile_pool(name="mx_pool", bufs=2))
         small = ctx.enter_context(tc.tile_pool(name="small", bufs=3))
-        psum_t = ctx.enter_context(tc.psum_pool(name="psum_t", bufs=2 * AHEAD + 1))
+        psum_t = ctx.enter_context(tc.psum_pool(name="psum_t", bufs=BANKS + 1))
         psum_norm = ctx.enter_context(tc.psum_pool(name="psum_norm", bufs=2))
         psum_acc = ctx.enter_context(tc.psum_pool(name="psum_acc", bufs=1))
 
@@ -98,6 +97,7 @@ def tile_npertokenswishglu_basis_pa_k_kernel(
             for b in range(BANKS):
                 passes = slice(PER_BANK * b, PER_BANK * (b + 1))
                 nc.sync.dma_start(out=w_raw[:, passes, :], in_=w_rows[:, passes, :])
+            for b in range(BANKS):
                 first = g * (FEATURES // 2) + b * piece
                 nc.sync.dma_start(
                     out=x_raw[:, b * piece : (b + 1) * piece],
@@ -106,20 +106,18 @@ def tile_npertokenswishglu_basis_pa_k_kernel(
             w_raw_of[unit] = w_raw
             x_raw_of[unit] = x_raw
 
-        def fill_w(bank):
-            unit, b = divmod(bank, BANKS)
+        def fill_w(unit, b):
             words = w_raw_of[unit][:].bitcast(F32)
             w_bank = psum_t.tile([P, PER_BANK, P], F32, tag="bank")
             for i in range(PER_BANK):
                 nc.tensor.transpose(w_bank[:, i, :], words[:, PER_BANK * b + i, :], ident[:])
-            w_bank_of[bank] = w_bank
+            w_bank_of[unit, b] = w_bank
 
-        def square_w(bank):
-            unit, b = divmod(bank, BANKS)
+        def square_w(unit, b):
             if b == 0:
                 partial = small.tile([P, 2, BANKS], F32)
                 partial_of[unit] = partial
-            by_parity = w_bank_of[bank][:].bitcast(BF16).rearrange("k i (p e) -> k e i p", e=2)
+            by_parity = w_bank_of[unit, b][:].bitcast(BF16).rearrange("k i (p e) -> k e i p", e=2)
             for e in range(2):
                 squares = small.tile([P, PER_BANK, P], BF16)
                 nc.scalar.activation(
@@ -129,8 +127,7 @@ def tile_npertokenswishglu_basis_pa_k_kernel(
                     accum_out=partial_of[unit][:, e, b : b + 1],
                 )
 
-        def fill_x(bank):
-            unit, b = divmod(bank, BANKS)
+        def fill_x(unit, b):
             words = x_raw_of[unit][:].bitcast(F32)
             x_bank = psum_t.tile([P, PER_BANK, BATCH], F32, tag="bank")
             for i in range(PER_BANK // 2):
@@ -139,27 +136,19 @@ def tile_npertokenswishglu_basis_pa_k_kernel(
                     nc.tensor.transpose(
                         x_bank[:, 2 * i + j, :], words[:, first + j : first + 2 * P : 2], ident[:]
                     )
-            x_bank_of[bank] = x_bank
+            x_bank_of[unit, b] = x_bank
 
-        def copy_x(bank):
-            unit, b = divmod(bank, BANKS)
+        def copy_x(unit, b):
             if b == 0:
                 x_grouped = grouped_pool.tile([P, HALF, BATCH, PACK], BF16, align_bytes=64)
                 x_grouped_of[unit] = x_grouped
             passes = slice(b * (PER_BANK // 2), (b + 1) * (PER_BANK // 2))
-            nc.scalar.copy(
-                out=x_grouped_of[unit][:].bitcast(F32)[:, passes, :, :],
-                in_=x_bank_of[bank][:].rearrange("p (i j) b -> p i b j", j=2),
-            )
-
-        def banks(first, count):
-            for bank in range(first, first + count):
-                if bank + AHEAD < ALL_BANKS:
-                    fill_w(bank + AHEAD)
-                square_w(bank)
-                if bank + AHEAD < ALL_BANKS:
-                    fill_x(bank + AHEAD)
-                copy_x(bank)
+            words_out = x_grouped_of[unit][:].bitcast(F32)[:, passes, :, :]
+            words_in = x_bank_of[unit, b][:].rearrange("p (i j) b -> p i b j", j=2)
+            if unit < VECTOR_COPIES:
+                nc.vector.tensor_copy(out=words_out, in_=words_in)
+            else:
+                nc.scalar.copy(out=words_out, in_=words_in)
 
         def fold_partial_sums(unit):
             norm_ps = psum_norm.tile([P, 2 * HIDDEN], F32)
@@ -280,30 +269,35 @@ def tile_npertokenswishglu_basis_pa_k_kernel(
             )
             nc.sync.dma_start(out=out[:, token, :], in_=result[:])
 
+        def square_banks(unit, first, count):
+            for b in range(first, first + count):
+                fill_x(unit, b)
+                square_w(unit, b)
+
+        def copy_banks(unit):
+            for b in range(BANKS):
+                if unit + 1 < UNITS:
+                    fill_w(unit + 1, b)
+                copy_x(unit, b)
+
         def pipeline():
             for unit in range(LOADED_AHEAD):
                 load(unit)
-            for bank in range(AHEAD):
-                fill_w(bank)
-                fill_x(bank)
+            for b in range(BANKS):
+                fill_w(0, b)
             for step in range(UNITS + 3):
                 measuring = step < UNITS
                 normalising = 1 <= step <= UNITS
                 unit = step - 1
                 token, g = divmod(unit, MATS)
+                finishing = step >= 4 and g == 1
 
+                if finishing:
+                    multiply(token - 1)
                 if measuring:
-                    banks(step * BANKS, BANKS // 2)
+                    square_banks(step, 0, 1)
                 if normalising:
                     spread_inverse_norms(unit)
-                if step >= 4 and g == 1:
-                    finish(token - 1)
-                if measuring:
-                    banks(step * BANKS + BANKS // 2, BANKS // 2)
-                    fold_partial_sums(step)
-                if step >= 3 and g == 0:
-                    multiply(token - 1)
-                if normalising:
                     if g == 0:
                         for h in range(2):
                             w_grouped = grouped_pool.tile(
@@ -315,13 +309,17 @@ def tile_npertokenswishglu_basis_pa_k_kernel(
                     normalise(
                         nc.gpsimd, inv_norm_of[unit][:], unit, HALF - GPSIMD_PASSES, GPSIMD_PASSES
                     )
+                if finishing:
+                    apply_gains(token - 1)
                 if measuring:
+                    square_banks(step, 1, BANKS - 1)
+                    fold_partial_sums(step)
                     inverse_norms(step)
+                    copy_banks(step)
+                if finishing:
+                    finish(token - 1)
                 if normalising:
                     normalise(nc.vector, in_psum, unit, HALF, HALF)
-                if step >= 3 and g == 0:
-                    apply_gains(token - 1)
-                if normalising:
                     quantise_x(unit)
                     if g == 1:
                         quantise_w(token)

@@ -24,7 +24,8 @@ PER_BANK = 4
 BANKS = PASSES // PER_BANK
 VECTOR_COPIES = 2
 LOADED_AHEAD = 6
-GPSIMD_PASSES = 4
+X_PIECES = 2
+GPSIMD_PASSES = 3
 EPS = 1e-12
 
 FLOPS = 2 * BATCH * TOKENS * FEATURES * MATS * HIDDEN
@@ -93,11 +94,11 @@ def tile_npertokenswishglu_basis_pa_k_kernel(
             w_rows = w[token, :, :].rearrange("(c p t) f -> p c (t f)", p=P, t=PACK)
             w_raw = raw_pool.tile([P, PASSES, PACK * HIDDEN], BF16)
             x_raw = raw_pool.tile([P, FEATURES // 2], BF16)
-            piece = FEATURES // 2 // BANKS
+            piece = FEATURES // 2 // X_PIECES
             for b in range(BANKS):
                 passes = slice(PER_BANK * b, PER_BANK * (b + 1))
                 nc.sync.dma_start(out=w_raw[:, passes, :], in_=w_rows[:, passes, :])
-            for b in range(BANKS):
+            for b in range(X_PIECES):
                 first = g * (FEATURES // 2) + b * piece
                 nc.sync.dma_start(
                     out=x_raw[:, b * piece : (b + 1) * piece],

@@ -321,7 +321,9 @@ def tile_npertokenswishglu_basis_pa_k_kernel(
                     finish(token - 1)
                 if normalising:
                     normalise(nc.vector, in_psum, unit, HALF, HALF)
-                    quantise_x(unit)
+                if measuring:
+                    quantise_x(step)
+                if normalising:
                     if g == 1:
                         quantise_w(token)
                     if unit + LOADED_AHEAD < UNITS:

@@ -51,8 +51,6 @@ def tile_npertokenswishglu_basis_pa_k_kernel(
 
         ident = consts.tile([P, P], F32)
         make_identity(nc, ident[:])
-        ones = consts.tile([P, P], F32)
-        nc.vector.memset(ones[:], 1.0)
         minus_half = consts.tile([P, 2], F32)
         nc.vector.memset(minus_half[:], -0.5)
         fold_q = consts.tile([P, HIDDEN_PAIRS], F32)
@@ -83,7 +81,7 @@ def tile_npertokenswishglu_basis_pa_k_kernel(
 
         w_raw_of, x_raw_of = {}, {}
         w_bank_of, x_bank_of = {}, {}
-        partial_of, norm_ps_of, diag_of, inv_norm_of = {}, {}, {}, {}
+        partial_of, norm_ps_of, inv_of, inv_norm_of = {}, {}, {}, {}
         x_grouped_of, w_grouped_of = {}, {}
         x_mx_of, w_mx_of = {}, {}
         acc_of, scaled_of = {}, {}
@@ -174,24 +172,18 @@ def tile_npertokenswishglu_basis_pa_k_kernel(
             nc.gpsimd.tensor_scalar_max(out=floored[:], in0=sum_sq[:], scalar1=EPS * EPS)
             inv = small.tile([P, 2], F32)
             nc.gpsimd.tensor_tensor(out=inv[:], in0=floored[:], in1=minus_half[:], op=ALU.pow)
-            diag = small.tile([P, HIDDEN_PAIRS, 2], F32)
-            nc.gpsimd.tensor_tensor(
-                out=diag[:],
-                in0=ident[:, 0:HIDDEN_PAIRS].unsqueeze(2).to_broadcast([P, HIDDEN_PAIRS, 2]),
-                in1=inv[:].unsqueeze(1).to_broadcast([P, HIDDEN_PAIRS, 2]),
-                op=ALU.mult,
-            )
-            diag_of[unit] = diag
+            inv_of[unit] = inv
 
         def spread_inverse_norms(unit):
             spread = norm_ps_of[unit][:, HIDDEN : 2 * HIDDEN]
-            nc.tensor.matmul(
-                out=spread,
-                lhsT=ones[:],
-                rhs=diag_of[unit][:].rearrange("k q e -> k (q e)"),
-                start=True,
-                stop=True,
-            )
+            for e in range(2):
+                nc.tensor.matmul(
+                    out=spread.rearrange("m (q e) -> m q e", e=2)[:, :, e],
+                    lhsT=inv_of[unit][:, e : e + 1].to_broadcast([P, P]),
+                    rhs=ident[:, 0:HIDDEN_PAIRS],
+                    start=True,
+                    stop=True,
+                )
             inv_norm = small.tile([P, HIDDEN], F32)
             nc.vector.tensor_copy(out=inv_norm[:], in_=spread)
             inv_norm_of[unit] = inv_norm

@@ -26,7 +26,10 @@ VECTOR_COPIES = 2
 LOADED_AHEAD = 6
 X_PIECES = 2
 GPSIMD_PASSES = 3
+RUN = 4
 EPS = 1e-12
+NW = 512
+FIRST_SPREAD = 1
 
 FLOPS = 2 * BATCH * TOKENS * FEATURES * MATS * HIDDEN
 
@@ -150,7 +153,7 @@ def tile_npertokenswishglu_basis_pa_k_kernel(
                 nc.scalar.copy(out=words_out, in_=words_in)
 
         def fold_partial_sums(unit):
-            norm_ps = psum_norm.tile([P, 2 * HIDDEN], F32)
+            norm_ps = psum_norm.tile([P, NW], F32)
             nc.tensor.matmul(
                 out=norm_ps[:, 0 : 2 * BANKS],
                 lhsT=fold[:].rearrange("k t q -> k (t q)"),
@@ -184,21 +187,28 @@ def tile_npertokenswishglu_basis_pa_k_kernel(
                     start=True,
                     stop=True,
                 )
+
+        def copy_inverse_norms(unit):
             inv_norm = small.tile([P, HIDDEN], F32)
-            nc.vector.tensor_copy(out=inv_norm[:], in_=spread)
+            nc.vector.tensor_copy(
+                out=inv_norm[:], in_=norm_ps_of[unit][:, HIDDEN : 2 * HIDDEN]
+            )
             inv_norm_of[unit] = inv_norm
 
         def normalise(engine, inv_norm, unit, first, count):
             token, g = divmod(unit, MATS)
-            h, c = divmod(first, HALF)
-            engine.tensor_tensor(
-                out=w_grouped_of[token, h][:, c : c + count, g, :, :],
-                in0=w_raw_of[unit][:, first : first + count, :].rearrange(
-                    "p c (t f) -> p c f t", t=PACK
-                ),
-                in1=inv_norm.unsqueeze(1).unsqueeze(3).to_broadcast([P, count, HIDDEN, PACK]),
-                op=ALU.mult,
-            )
+            for i in range(first, first + count):
+                h, c = divmod(i, HALF)
+                engine.tensor_tensor(
+                    out=w_grouped_of[token, h][:, c, g, :, :].rearrange(
+                        "p (q i) t -> p q t i", i=RUN
+                    ),
+                    in0=w_raw_of[unit][:, i, :].rearrange("p (t q i) -> p q t i", t=PACK, i=RUN),
+                    in1=inv_norm.rearrange("p (q i) -> p q i", i=RUN)
+                    .unsqueeze(2)
+                    .to_broadcast([P, HIDDEN // RUN, PACK, RUN]),
+                    op=ALU.mult,
+                )
 
         def quantise_x(unit):
             token, h = divmod(unit, MATS)
@@ -271,6 +281,8 @@ def tile_npertokenswishglu_basis_pa_k_kernel(
             for b in range(BANKS):
                 if unit + 1 < UNITS:
                     fill_w(unit + 1, b)
+                if unit == 0 and b == FIRST_SPREAD:
+                    spread_inverse_norms(0)
                 copy_x(unit, b)
 
         def pipeline():
@@ -290,7 +302,9 @@ def tile_npertokenswishglu_basis_pa_k_kernel(
                 if measuring:
                     square_banks(step, 0, 1)
                 if normalising:
-                    spread_inverse_norms(unit)
+                    if unit:
+                        spread_inverse_norms(unit)
+                    copy_inverse_norms(unit)
                     if g == 0:
                         for h in range(2):
                             w_grouped = grouped_pool.tile(

@@ -25,11 +25,10 @@ BANKS = PASSES // PER_BANK
 VECTOR_COPIES = 2
 LOADED_AHEAD = 6
 X_PIECES = 2
-GPSIMD_PASSES = 3
+GPSIMD_PASSES = 2
+BANK_WORDS = 512
 RUN = 4
 EPS = 1e-12
-NW = 512
-FIRST_SPREAD = 1
 
 FLOPS = 2 * BATCH * TOKENS * FEATURES * MATS * HIDDEN
 
@@ -54,6 +53,8 @@ def tile_npertokenswishglu_basis_pa_k_kernel(
 
         ident = consts.tile([P, P], F32)
         make_identity(nc, ident[:])
+        ones = consts.tile([P, P], F32)
+        nc.vector.memset(ones[:], 1.0)
         minus_half = consts.tile([P, 2], F32)
         nc.vector.memset(minus_half[:], -0.5)
         fold_q = consts.tile([P, HIDDEN_PAIRS], F32)
@@ -84,7 +85,7 @@ def tile_npertokenswishglu_basis_pa_k_kernel(
 
         w_raw_of, x_raw_of = {}, {}
         w_bank_of, x_bank_of = {}, {}
-        partial_of, norm_ps_of, inv_of, inv_norm_of = {}, {}, {}, {}
+        partial_of, norm_ps_of, inv_of, inv_norm_of, diagonal_of = {}, {}, {}, {}, {}
         x_grouped_of, w_grouped_of = {}, {}
         x_mx_of, w_mx_of = {}, {}
         acc_of, scaled_of = {}, {}
@@ -153,7 +154,7 @@ def tile_npertokenswishglu_basis_pa_k_kernel(
                 nc.scalar.copy(out=words_out, in_=words_in)
 
         def fold_partial_sums(unit):
-            norm_ps = psum_norm.tile([P, NW], F32)
+            norm_ps = psum_norm.tile([P, BANK_WORDS], F32)
             nc.tensor.matmul(
                 out=norm_ps[:, 0 : 2 * BANKS],
                 lhsT=fold[:].rearrange("k t q -> k (t q)"),
@@ -177,16 +178,24 @@ def tile_npertokenswishglu_basis_pa_k_kernel(
             nc.gpsimd.tensor_tensor(out=inv[:], in0=floored[:], in1=minus_half[:], op=ALU.pow)
             inv_of[unit] = inv
 
+        def place_inverse_norms(unit):
+            diagonal = small.tile([P, HIDDEN_PAIRS, 2], F32)
+            nc.gpsimd.tensor_tensor(
+                out=diagonal[:],
+                in0=ident[:, 0:HIDDEN_PAIRS].unsqueeze(2).to_broadcast([P, HIDDEN_PAIRS, 2]),
+                in1=inv_of[unit][:].unsqueeze(1).to_broadcast([P, HIDDEN_PAIRS, 2]),
+                op=ALU.mult,
+            )
+            diagonal_of[unit] = diagonal
+
         def spread_inverse_norms(unit):
-            spread = norm_ps_of[unit][:, HIDDEN : 2 * HIDDEN]
-            for e in range(2):
-                nc.tensor.matmul(
-                    out=spread.rearrange("m (q e) -> m q e", e=2)[:, :, e],
-                    lhsT=inv_of[unit][:, e : e + 1].to_broadcast([P, P]),
-                    rhs=ident[:, 0:HIDDEN_PAIRS],
-                    start=True,
-                    stop=True,
-                )
+            nc.tensor.matmul(
+                out=norm_ps_of[unit][:, HIDDEN : 2 * HIDDEN],
+                lhsT=ones[:],
+                rhs=diagonal_of[unit][:].rearrange("k q e -> k (q e)"),
+                start=True,
+                stop=True,
+            )
 
         def copy_inverse_norms(unit):
             inv_norm = small.tile([P, HIDDEN], F32)
@@ -227,12 +236,18 @@ def tile_npertokenswishglu_basis_pa_k_kernel(
         def quantise_w(token):
             w_codes = mx_pool.tile([P, PASSES, MATS * HIDDEN], U32, align_bytes=64)
             w_scales = mx_pool.tile([P, PASSES, MATS * HIDDEN], U8, align_bytes=64)
-            for h in range(2):
-                passes = slice(h * HALF, (h + 1) * HALF)
+            ends = [HALF, PASSES]
+            if token == TOKENS - 1:
+                ends = [HALF, HALF + HALF // 2, PASSES]
+            for first, end in zip([0] + ends, ends):
+                h, c = divmod(first, HALF)
+                passes = slice(first, end)
                 nc.vector.quantize_mx(
                     out=w_codes[:, passes, :].rearrange("p c n -> p (c n)").bitcast(FP8X4),
                     scales=w_scales[:, passes, :].rearrange("p c n -> p (c n)"),
-                    in_=w_grouped_of[token, h][:].rearrange("p c g f t -> p (c g f t)"),
+                    in_=w_grouped_of[token, h][:, c : c + end - first, :, :, :].rearrange(
+                        "p c g f t -> p (c g f t)"
+                    ),
                 )
             w_mx_of[token] = (w_codes, w_scales)
 
@@ -267,7 +282,8 @@ def tile_npertokenswishglu_basis_pa_k_kernel(
             silu_v = small.tile([BATCH, HIDDEN], F32)
             nc.scalar.activation(out=silu_v[:], in_=scaled[:, 1, :], func=ACT.Silu)
             result = small.tile([BATCH, HIDDEN], F32)
-            nc.gpsimd.tensor_tensor(
+            engine = nc.vector if token == TOKENS - 1 else nc.gpsimd
+            engine.tensor_tensor(
                 out=result[:], in0=silu_v[:], in1=scaled[:, 0, :], op=ALU.mult
             )
             nc.sync.dma_start(out=out[:, token, :], in_=result[:])
@@ -281,9 +297,9 @@ def tile_npertokenswishglu_basis_pa_k_kernel(
             for b in range(BANKS):
                 if unit + 1 < UNITS:
                     fill_w(unit + 1, b)
-                if unit == 0 and b == FIRST_SPREAD:
-                    spread_inverse_norms(0)
                 copy_x(unit, b)
+            if unit == 0:
+                spread_inverse_norms(0)
 
         def pipeline():
             for unit in range(LOADED_AHEAD):
@@ -322,6 +338,7 @@ def tile_npertokenswishglu_basis_pa_k_kernel(
                     square_banks(step, 1, BANKS - 1)
                     fold_partial_sums(step)
                     inverse_norms(step)
+                    place_inverse_norms(step)
                     copy_banks(step)
                 if finishing:
                     finish(token - 1)

from contextlib import ExitStack
import math

import concourse.mybir as mybir
from concourse.masks import make_identity

F32 = mybir.dt.float32
BF16 = mybir.dt.bfloat16
U32 = mybir.dt.uint32
U8 = mybir.dt.uint8
FP8X4 = mybir.dt.float8_e4m3fn_x4
ALU = mybir.AluOpType
ACT = mybir.ActivationFunctionType

P = 128
BATCH, TOKENS, FEATURES, HIDDEN = 128, 8, 8192, 64
MATS = 2
UNITS = TOKENS * MATS
PACK = 4
PASSES = FEATURES // (P * PACK)
HALF = PASSES // 2
HIDDEN_PAIRS = HIDDEN // 2
PER_BANK = 4
BANKS = PASSES // PER_BANK
VECTOR_COPIES = 2
LOADED_AHEAD = 6
X_PIECES = 2
GPSIMD_PASSES = 2
BANK_WORDS = 512
RUN = 4
EPS = 1e-12

FLOPS = 2 * BATCH * TOKENS * FEATURES * MATS * HIDDEN


def tile_npertokenswishglu_basis_pa_k_kernel(
    tc, x, w_gate_mix, w_up_mix, u_scale_param, v_scale_param, out
):
    nc = tc.nc
    with ExitStack() as ctx:
        consts = ctx.enter_context(tc.tile_pool(name="consts", bufs=1))
        raw_pool = ctx.enter_context(tc.tile_pool(name="raw_pool", bufs=LOADED_AHEAD))
        grouped_pool = ctx.enter_context(tc.tile_pool(name="grouped_pool", bufs=4))
        mx_pool = ctx.enter_context(tc.tile_pool(name="mx_pool", bufs=2))
        small = ctx.enter_context(tc.tile_pool(name="small", bufs=3))
        psum_t = ctx.enter_context(tc.psum_pool(name="psum_t", bufs=BANKS + 1))
        psum_norm = ctx.enter_context(tc.psum_pool(name="psum_norm", bufs=2))
        psum_acc = ctx.enter_context(tc.psum_pool(name="psum_acc", bufs=1))

        warm = consts.tile([P, 1], F32)
        nc.vector.memset(warm[:], 0.0)
        nc.scalar.activation(out=warm[:], in_=warm[:], func=ACT.Silu)

        ident = consts.tile([P, P], F32)
        make_identity(nc, ident[:])
        ones = consts.tile([P, P], F32)
        nc.vector.memset(ones[:], 1.0)
        minus_half = consts.tile([P, 2], F32)
        nc.vector.memset(minus_half[:], -0.5)
        fold_q = consts.tile([P, HIDDEN_PAIRS], F32)
        nc.vector.tensor_reduce(
            out=fold_q[:],
            in_=ident[:].rearrange("k (t q) -> k q t", q=HIDDEN_PAIRS),
            axis=mybir.AxisListType.X,
            op=ALU.add,
        )
        fold = consts.tile([P, PACK, HIDDEN_PAIRS], F32)
        nc.vector.tensor_copy(
            out=fold[:], in_=fold_q[:].unsqueeze(1).to_broadcast([P, PACK, HIDDEN_PAIRS])
        )

        params = consts.tile([P, MATS, HIDDEN], BF16)
        for g, param in enumerate((u_scale_param, v_scale_param)):
            nc.scalar.dma_start(
                out=params[:, g, :],
                in_=param.rearrange("o f -> (o f)").partition_broadcast(P),
            )
        gains = consts.tile([P, MATS, HIDDEN], F32)
        nc.vector.scalar_tensor_tensor(
            out=gains[:], in0=params[:], scalar=-1.0, in1=params[:], op0=ALU.mult, op1=ALU.max
        )
        nc.vector.tensor_scalar_mul(
            out=gains[:, 1, :], in0=gains[:, 1, :], scalar1=math.sqrt(FEATURES)
        )

        w_raw_of, x_raw_of = {}, {}
        w_bank_of, x_bank_of = {}, {}
        partial_of, norm_ps_of, inv_of, inv_norm_of, diagonal_of = {}, {}, {}, {}, {}
        x_grouped_of, w_grouped_of = {}, {}
        x_mx_of, w_mx_of = {}, {}
        acc_of, scaled_of = {}, {}

        def load(unit):
            token, g = divmod(unit, MATS)
            w = (w_gate_mix, w_up_mix)[g]
            w_rows = w[token, :, :].rearrange("(c p t) f -> p c (t f)", p=P, t=PACK)
            w_raw = raw_pool.tile([P, PASSES, PACK * HIDDEN], BF16)
            x_raw = raw_pool.tile([P, FEATURES // 2], BF16)
            piece = FEATURES // 2 // X_PIECES
            for b in range(BANKS):
                passes = slice(PER_BANK * b, PER_BANK * (b + 1))
                nc.sync.dma_start(out=w_raw[:, passes, :], in_=w_rows[:, passes, :])
            for b in range(X_PIECES):
                first = g * (FEATURES // 2) + b * piece
                nc.sync.dma_start(
                    out=x_raw[:, b * piece : (b + 1) * piece],
                    in_=x[:, token, first : first + piece],
                )
            w_raw_of[unit] = w_raw
            x_raw_of[unit] = x_raw

        def fill_w(unit, b):
            words = w_raw_of[unit][:].bitcast(F32)
            w_bank = psum_t.tile([P, PER_BANK, P], F32, tag="bank")
            for i in range(PER_BANK):
                nc.tensor.transpose(w_bank[:, i, :], words[:, PER_BANK * b + i, :], ident[:])
            w_bank_of[unit, b] = w_bank

        def square_w(unit, b):
            if b == 0:
                partial = small.tile([P, 2, BANKS], F32)
                partial_of[unit] = partial
            by_parity = w_bank_of[unit, b][:].bitcast(BF16).rearrange("k i (p e) -> k e i p", e=2)
            for e in range(2):
                squares = small.tile([P, PER_BANK, P], BF16)
                nc.scalar.activation(
                    out=squares[:],
                    in_=by_parity[:, e, :, :],
                    func=ACT.Square,
                    accum_out=partial_of[unit][:, e, b : b + 1],
                )

        def fill_x(unit, b):
            words = x_raw_of[unit][:].bitcast(F32)
            x_bank = psum_t.tile([P, PER_BANK, BATCH], F32, tag="bank")
            for i in range(PER_BANK // 2):
                first = 2 * P * (b * (PER_BANK // 2) + i)
                for j in range(2):
                    nc.tensor.transpose(
                        x_bank[:, 2 * i + j, :], words[:, first + j : first + 2 * P : 2], ident[:]
                    )
            x_bank_of[unit, b] = x_bank

        def copy_x(unit, b):
            if b == 0:
                x_grouped = grouped_pool.tile([P, HALF, BATCH, PACK], BF16, align_bytes=64)
                x_grouped_of[unit] = x_grouped
            passes = slice(b * (PER_BANK // 2), (b + 1) * (PER_BANK // 2))
            words_out = x_grouped_of[unit][:].bitcast(F32)[:, passes, :, :]
            words_in = x_bank_of[unit, b][:].rearrange("p (i j) b -> p i b j", j=2)
            if unit < VECTOR_COPIES:
                nc.vector.tensor_copy(out=words_out, in_=words_in)
            else:
                nc.scalar.copy(out=words_out, in_=words_in)

        def fold_partial_sums(unit):
            norm_ps = psum_norm.tile([P, BANK_WORDS], F32)
            nc.tensor.matmul(
                out=norm_ps[:, 0 : 2 * BANKS],
                lhsT=fold[:].rearrange("k t q -> k (t q)"),
                rhs=partial_of[unit][:].rearrange("k e b -> k (e b)"),
                start=True,
                stop=True,
            )
            norm_ps_of[unit] = norm_ps

        def inverse_norms(unit):
            sum_sq = small.tile([P, 2], F32)
            nc.vector.tensor_reduce(
                out=sum_sq[:],
                in_=norm_ps_of[unit][:, 0 : 2 * BANKS].rearrange("k (e b) -> k e b", e=2),
                axis=mybir.AxisListType.X,
                op=ALU.add,
            )
            floored = small.tile([P, 2], F32)
            nc.gpsimd.tensor_scalar_max(out=floored[:], in0=sum_sq[:], scalar1=EPS * EPS)
            inv = small.tile([P, 2], F32)
            nc.gpsimd.tensor_tensor(out=inv[:], in0=floored[:], in1=minus_half[:], op=ALU.pow)
            inv_of[unit] = inv

        def place_inverse_norms(unit):
            diagonal = small.tile([P, HIDDEN_PAIRS, 2], F32)
            nc.gpsimd.tensor_tensor(
                out=diagonal[:],
                in0=ident[:, 0:HIDDEN_PAIRS].unsqueeze(2).to_broadcast([P, HIDDEN_PAIRS, 2]),
                in1=inv_of[unit][:].unsqueeze(1).to_broadcast([P, HIDDEN_PAIRS, 2]),
                op=ALU.mult,
            )
            diagonal_of[unit] = diagonal

        def spread_inverse_norms(unit):
            nc.tensor.matmul(
                out=norm_ps_of[unit][:, HIDDEN : 2 * HIDDEN],
                lhsT=ones[:],
                rhs=diagonal_of[unit][:].rearrange("k q e -> k (q e)"),
                start=True,
                stop=True,
            )

        def copy_inverse_norms(unit):
            inv_norm = small.tile([P, HIDDEN], F32)
            nc.vector.tensor_copy(
                out=inv_norm[:], in_=norm_ps_of[unit][:, HIDDEN : 2 * HIDDEN]
            )
            inv_norm_of[unit] = inv_norm

        def normalise(engine, inv_norm, unit, first, count):
            token, g = divmod(unit, MATS)
            for i in range(first, first + count):
                h, c = divmod(i, HALF)
                engine.tensor_tensor(
                    out=w_grouped_of[token, h][:, c, g, :, :].rearrange(
                        "p (q i) t -> p q t i", i=RUN
                    ),
                    in0=w_raw_of[unit][:, i, :].rearrange("p (t q i) -> p q t i", t=PACK, i=RUN),
                    in1=inv_norm.rearrange("p (q i) -> p q i", i=RUN)
                    .unsqueeze(2)
                    .to_broadcast([P, HIDDEN // RUN, PACK, RUN]),
                    op=ALU.mult,
                )

        def quantise_x(unit):
            token, h = divmod(unit, MATS)
            if h == 0:
                x_codes = mx_pool.tile([P, PASSES, BATCH], U32, align_bytes=64)
                x_scales = mx_pool.tile([P, PASSES, BATCH], U8, align_bytes=64)
                x_mx_of[token] = (x_codes, x_scales)
            x_codes, x_scales = x_mx_of[token]
            passes = slice(h * HALF, (h + 1) * HALF)
            nc.vector.quantize_mx(
                out=x_codes[:, passes, :].rearrange("p c b -> p (c b)").bitcast(FP8X4),
                scales=x_scales[:, passes, :].rearrange("p c b -> p (c b)"),
                in_=x_grouped_of[unit][:].rearrange("p c b t -> p (c b t)"),
            )

        def quantise_w(token):
            w_codes = mx_pool.tile([P, PASSES, MATS * HIDDEN], U32, align_bytes=64)
            w_scales = mx_pool.tile([P, PASSES, MATS * HIDDEN], U8, align_bytes=64)
            ends = [HALF, PASSES]
            if token == TOKENS - 1:
                ends = [HALF, HALF + HALF // 2, PASSES]
            for first, end in zip([0] + ends, ends):
                h, c = divmod(first, HALF)
                passes = slice(first, end)
                nc.vector.quantize_mx(
                    out=w_codes[:, passes, :].rearrange("p c n -> p (c n)").bitcast(FP8X4),
                    scales=w_scales[:, passes, :].rearrange("p c n -> p (c n)"),
                    in_=w_grouped_of[token, h][:, c : c + end - first, :, :, :].rearrange(
                        "p c g f t -> p (c g f t)"
                    ),
                )
            w_mx_of[token] = (w_codes, w_scales)

        def multiply(token):
            x_codes, x_scales = x_mx_of[token]
            w_codes, w_scales = w_mx_of[token]
            acc = psum_acc.tile([BATCH, MATS * HIDDEN], F32)
            for c in range(PASSES):
                nc.tensor.matmul_mx(
                    out=acc[:],
                    lhsT=x_codes[:, c, :].bitcast(FP8X4),
                    lhsT_scale=x_scales[:, c, :],
                    rhs=w_codes[:, c, :].bitcast(FP8X4),
                    rhs_scale=w_scales[:, c, :],
                    start=(c == 0),
                    stop=(c == PASSES - 1),
                )
            acc_of[token] = acc

        def apply_gains(token):
            scaled = small.tile([BATCH, MATS, HIDDEN], F32)
            nc.vector.tensor_tensor(
                out=scaled[:],
                in0=acc_of[token][:].rearrange("b (g f) -> b g f", g=MATS),
                in1=gains[:],
                op=ALU.mult,
            )
            scaled_of[token] = scaled

        def finish(token):
            scaled = scaled_of[token]
            silu_v = small.tile([BATCH, HIDDEN], F32)
            nc.scalar.activation(out=silu_v[:], in_=scaled[:, 1, :], func=ACT.Silu)
            result = small.tile([BATCH, HIDDEN], F32)
            engine = nc.vector if token == TOKENS - 1 else nc.gpsimd
            engine.tensor_tensor(
                out=result[:], in0=silu_v[:], in1=scaled[:, 0, :], op=ALU.mult
            )
            nc.sync.dma_start(out=out[:, token, :], in_=result[:])

        def square_banks(unit, first, count):
            for b in range(first, first + count):
                fill_x(unit, b)
                square_w(unit, b)

        def copy_banks(unit):
            for b in range(BANKS):
                if unit + 1 < UNITS:
                    fill_w(unit + 1, b)
                copy_x(unit, b)
            if unit == 0:
                spread_inverse_norms(0)

        def pipeline():
            for unit in range(LOADED_AHEAD):
                load(unit)
            for b in range(BANKS):
                fill_w(0, b)
            for step in range(UNITS + 3):
                measuring = step < UNITS
                normalising = 1 <= step <= UNITS
                unit = step - 1
                token, g = divmod(unit, MATS)
                finishing = step >= 4 and g == 1

                if finishing:
                    multiply(token - 1)
                if measuring:
                    square_banks(step, 0, 1)
                if normalising:
                    if unit:
                        spread_inverse_norms(unit)
                    copy_inverse_norms(unit)
                    if g == 0:
                        for h in range(2):
                            w_grouped = grouped_pool.tile(
                                [P, HALF, MATS, HIDDEN, PACK], BF16, align_bytes=64
                            )
                            w_grouped_of[token, h] = w_grouped
                    in_psum = norm_ps_of[unit][:, HIDDEN : 2 * HIDDEN]
                    normalise(nc.vector, in_psum, unit, 0, HALF - GPSIMD_PASSES)
                    normalise(
                        nc.gpsimd, inv_norm_of[unit][:], unit, HALF - GPSIMD_PASSES, GPSIMD_PASSES
                    )
                if finishing:
                    apply_gains(token - 1)
                if measuring:
                    square_banks(step, 1, BANKS - 1)
                    fold_partial_sums(step)
                    inverse_norms(step)
                    place_inverse_norms(step)
                    copy_banks(step)
                if finishing:
                    finish(token - 1)
                if normalising:
                    normalise(nc.vector, in_psum, unit, HALF, HALF)
                if measuring:
                    quantise_x(step)
                if normalising:
                    if g == 1:
                        quantise_w(token)
                    if unit + LOADED_AHEAD < UNITS:
                        load(unit + LOADED_AHEAD)

        with tc.manual_schedule():
            pipeline()
